import numpy as np
import ml_dtypes


def mxq(x, axis, fmt="e4m3"):
    dtype, down = {"e4m3": (ml_dtypes.float8_e4m3fn, 7), "e5m2": (ml_dtypes.float8_e5m2, 14)}[fmt]
    v = np.moveaxis(np.asarray(x, np.float32).astype(ml_dtypes.bfloat16).astype(np.float64), axis, -1)
    blocks = v.reshape(v.shape[:-1] + (-1, 32))
    amax = np.abs(blocks).max(-1, keepdims=True)
    byte = np.maximum(np.where(amax > 0, np.frexp(amax)[1] - 1 + 127, 0) - down, 1)
    scale = np.exp2(byte - 127.0)
    codes = (blocks / scale).astype(np.float32).astype(dtype).astype(np.float64)
    return np.moveaxis((codes * scale).reshape(v.shape), -1, axis)


WIDE = False


def mx_kscale(k):
    if not WIDE:
        return np.ones(k)
    levels = np.array([30, -30])
    if k % 512:
        return np.exp2(np.random.permutation(np.resize(levels, k // 32))).repeat(32)
    a = np.empty((k // 512, 16))
    for p in range(k // 512):
        a[p, :8] = np.random.permutation(np.resize(levels, 8))
        for g in range(8):
            far = levels[np.abs(levels - a[p, g]) >= 10]
            a[p, g + 8] = far[np.random.randint(len(far))]
    return np.exp2(a.ravel()).repeat(32)


BF16 = ml_dtypes.bfloat16


def bf(x):
    return np.asarray(x, np.float32).astype(BF16)


def f64(x):
    return np.asarray(x).astype(np.float64)


B, S, DIM, H, HKV, HD, RD, TRAIN_SEQ = 2, 256, 2048, 16, 4, 128, 64, 128
E, EKV, HALF = H * HD, HKV * HD, RD // 2
BASE = 10000.0
EPS = 1.1920929e-07


def rope_tables():
    if S > TRAIN_SEQ:
        base = BASE * (S / TRAIN_SEQ) ** (RD / (RD - 2))
    else:
        base = BASE
    inv_freq = 1.0 / base ** (np.arange(0, RD, 2) / RD)
    freqs = np.outer(np.arange(S), inv_freq)
    return np.cos(freqs), np.sin(freqs)


def rms_norm(u):
    return u / np.sqrt(np.mean(np.square(u), axis=-1, keepdims=True) + EPS)


def apply_rope(u, cos, sin):
    c = cos[None, :, None, :]
    sn = sin[None, :, None, :]
    u1, u2, u_pass = u[..., :HALF], u[..., HALF:RD], u[..., RD:]
    return np.concatenate([u1 * c + u2 * sn, -u1 * sn + u2 * c, u_pass], axis=-1)


def setup_inputs():
    s = mx_kscale(DIM)
    c, sn = rope_tables()
    return {"x": bf(np.random.standard_normal((B, S, DIM)) * s),
            "Wq": bf(np.random.standard_normal((E, DIM)) / np.sqrt(DIM) / s),
            "Wk": bf(np.random.standard_normal((EKV, DIM)) / np.sqrt(DIM) / s),
            "Wv": bf(np.random.standard_normal((EKV, DIM)) / np.sqrt(DIM) / s),
            "q_gain": bf(1.0 + 0.1 * np.random.standard_normal(H)),
            "cos_tab": bf(c), "sin_tab": bf(sn)}


def reference(x, Wq, Wk, Wv, q_gain, cos_tab, sin_tab):
    xq = mxq(f64(x), 2, "e5m2")
    q = (xq @ mxq(f64(Wq), 1, "e5m2").T).reshape(B, S, H, HD)
    k = (xq @ mxq(f64(Wk), 1, "e5m2").T).reshape(B, S, HKV, HD)
    v = (xq @ mxq(f64(Wv), 1, "e5m2").T).reshape(B, S, HKV, HD)
    c, sn = f64(cos_tab), f64(sin_tab)
    q = apply_rope(rms_norm(q), c, sn) * f64(q_gain)[None, None, :, None]
    k = apply_rope(rms_norm(k), c, sn)
    return q, k, v

@@ -1,0 +1,227 @@
+from contextlib import ExitStack
+
+import concourse.mybir as mybir
+from concourse.masks import make_identity
+
+B, S, DIM, H, HKV, HD = 2, 256, 2048, 16, 4, 128
+HALF = 32
+EPS = 1.1920929e-07
+FLOPS = 2 * B * S * DIM * (H + 2 * HKV) * HD
+
+F32 = mybir.dt.float32
+BF16 = mybir.dt.bfloat16
+U32 = mybir.dt.uint32
+U8 = mybir.dt.uint8
+E5M2X4 = mybir.dt.float8_e5m2_x4
+ACT = mybir.ActivationFunctionType
+ALU = mybir.AluOpType
+
+P = 128
+K_PASS = 512
+PASSES = DIM // K_PASS
+ROWS = 512
+ROW_TILES = ROWS // P
+HEADS = ROWS // HD
+WORDS = K_PASS // 2
+
+
+def tile_causalselfattention_pa_kernel(tc, x, Wq, Wk, Wv, q_gain, cos_tab, sin_tab, out_0, out_1, out_2):
+    nc = tc.nc
+    x2 = x.rearrange("b s k -> (b s) k")
+    q2 = out_0.rearrange("b s h d -> (b s) (h d)")
+    k2 = out_1.rearrange("b s h d -> (b s) (h d)")
+    v2 = out_2.rearrange("b s h d -> (b s) (h d)")
+    chunks = [("k", Wk, k2, None)]
+    for c in range(H // HEADS):
+        chunks.append(("q", Wq[c * ROWS:(c + 1) * ROWS, :], q2[:, c * ROWS:(c + 1) * ROWS], c * HEADS))
+    chunks.append(("v", Wv, v2, None))
+    n_chunks = len(chunks)
+
+    with ExitStack() as ctx:
+        keep = ctx.enter_context(tc.tile_pool(name="keep", bufs=1))
+        work = ctx.enter_context(tc.tile_pool(name="work", bufs=1))
+        psum = ctx.enter_context(tc.psum_pool(name="psum", bufs=4))
+        ctx.enter_context(tc.manual_schedule())
+
+        ident = keep.tile([P, P], F32, name="ident")
+        make_identity(nc, ident[:])
+        cos_ext = keep.tile([P, 2, HD], F32, name="cos_ext")
+        sin_ext = keep.tile([P, 2, 2 * HALF], F32, name="sin_ext")
+        nc.gpsimd.memset(cos_ext[:, :, 2 * HALF:], 1.0)
+
+        def load(name, rows, g0, n_pass):
+            raw = keep.tile([P, ROW_TILES, n_pass * K_PASS], BF16, name=name)
+            cols = slice(g0 * K_PASS, (g0 + n_pass) * K_PASS)
+            nc.sync.dma_start(out=raw[:], in_=rows[:, cols].rearrange("(r p) k -> p r k", p=P))
+            words = raw[:].bitcast(F32)
+            return [words[:, :, i * WORDS:(i + 1) * WORDS] for i in range(n_pass)]
+
+        units = []
+        for g in range(PASSES):
+            units.append((("x", g), load("x_raw%d" % g, x2, g, 1)[0]))
+            units.append(((0, g), load("w0_raw%d" % g, chunks[0][1], g, 1)[0]))
+        cos_raw = keep.tile([P, 2, HALF], BF16, name="cos_raw")
+        sin_raw = keep.tile([P, 2, HALF], BF16, name="sin_raw")
+        nc.sync.dma_start(out=cos_raw[:], in_=cos_tab.rearrange("(j p) d -> p j d", p=P))
+        nc.sync.dma_start(out=sin_raw[:], in_=sin_tab.rearrange("(j p) d -> p j d", p=P))
+        gain = keep.tile([P, H], BF16, name="gain")
+        for c in range(1, n_chunks):
+            for g0 in (0, 2):
+                pair = load("w%d_raw%d" % (c, g0), chunks[c][1], g0, 2)
+                units.append(((c, g0), pair[0]))
+                units.append(((c, g0 + 1), pair[1]))
+            if c == 1:
+                nc.sync.dma_start(out=gain[:], in_=q_gain.partition_broadcast(P))
+
+        nc.gpsimd.tensor_copy(out=cos_ext[:, :, 0:HALF], in_=cos_raw[:])
+        nc.gpsimd.tensor_copy(out=cos_ext[:, :, HALF:2 * HALF], in_=cos_raw[:])
+        nc.gpsimd.tensor_copy(out=sin_ext[:, :, 0:HALF], in_=sin_raw[:])
+        nc.gpsimd.tensor_scalar(out=sin_ext[:, :, HALF:], in0=sin_raw[:], scalar1=-1.0, scalar2=0.0,
+                                op0=ALU.mult, op1=ALU.add)
+
+        banks, grouped, quantised = {}, {}, {}
+        acc, stage, swapped, ssq, rstd, factor = {}, {}, {}, {}, {}, {}
+
+        def transpose_unit(j):
+            words = units[j][1]
+            for b in range(2):
+                bank = psum.tile([P, 2, 2, P], F32, name="bank", tag="bank")
+                banks[j, b] = bank
+                for r in range(2):
+                    for u in range(2):
+                        nc.tensor.transpose(bank[:, r, u, :], words[:, 2 * b + r, u:WORDS:2], ident[:])
+
+        def drain(j, b):
+            if b == 0:
+                grouped[j] = work.tile([P, 4 * ROWS], BF16, name="grouped", tag="grouped", bufs=4, align_bytes=64)
+            dst = grouped[j][:].bitcast(F32)[:, b * ROWS:(b + 1) * ROWS]
+            nc.scalar.copy(out=dst.rearrange("p (r n u) -> p r n u", r=2, u=2),
+                           in_=banks[j, b][:].rearrange("p r u n -> p r n u"))
+
+        def quantise(j):
+            key = units[j][0]
+            tag, bufs = ("x", PASSES) if key[0] == "x" else ("w", 10)
+            codes = work.tile([P, ROWS], U32, name=tag + "_codes", tag=tag + "_codes", bufs=bufs, align_bytes=64)
+            scales = work.tile([P, ROWS], U8, name=tag + "_scales", tag=tag + "_scales", bufs=bufs, align_bytes=64)
+            nc.vector.quantize_mx(out=codes[:].bitcast(E5M2X4), scales=scales[:], in_=grouped[j][:])
+            quantised[key] = (codes, scales)
+
+        def multiply(i, g):
+            c, t = divmod(i, ROW_TILES)
+            if g == 0:
+                acc[i] = psum.tile([P, ROWS], F32, name="acc", tag="acc")
+            x_codes, x_scales = quantised["x", g]
+            w_codes, w_scales = quantised[c, g]
+            tokens = slice(t * P, (t + 1) * P)
+            nc.tensor.matmul_mx(out=acc[i][:], lhsT=x_codes[:, tokens].bitcast(E5M2X4), lhsT_scale=x_scales[:, tokens],
+                                rhs=w_codes[:].bitcast(E5M2X4), rhs_scale=w_scales[:],
+                                start=(g == 0), stop=(g == PASSES - 1))
+
+        def kind(i):
+            return chunks[i // ROW_TILES][0]
+
+        def store(i):
+            c, t = divmod(i, ROW_TILES)
+            nc.sync.dma_start(out=chunks[c][2][t * P:(t + 1) * P, :], in_=stage[i][:])
+
+        def scalar_read(i):
+            stage[i] = work.tile([P, ROWS], F32, name="stage", tag="stage", bufs=12)
+            if kind(i) == "v":
+                nc.scalar.copy(out=stage[i][:], in_=acc[i][:])
+                store(i)
+                return
+            pair, side = divmod(i, 2)
+            if side == 0:
+                ssq[pair] = work.tile([P, 2 * HEADS], F32, name="ssq", tag="ssq", bufs=3)
+            for h in range(HEADS):
+                col = side * HEADS + h
+                nc.scalar.activation(out=stage[i][:, h * HD:(h + 1) * HD], in_=acc[i][:, h * HD:(h + 1) * HD],
+                                     func=ACT.Square, accum_out=ssq[pair][:, col:col + 1])
+
+        def inverse_rms(pair):
+            rstd[pair] = work.tile([P, 2 * HEADS], F32, name="rstd", tag="rstd", bufs=3)
+            nc.scalar.activation(out=rstd[pair][:], in_=ssq[pair][:], func=ACT.Abs_reciprocal_sqrt,
+                                 scale=1.0 / HD, bias=EPS)
+
+        def sine_terms(i):
+            j = i % 2
+            u = acc[i][:].rearrange("p (h d) -> p h d", h=HEADS)
+            swapped[i] = work.tile([P, HEADS, 2 * HALF], F32, name="swapped", tag="swapped", bufs=4)
+            nc.vector.tensor_tensor(out=swapped[i][:, :, 0:HALF], in0=u[:, :, HALF:2 * HALF],
+                                    in1=sin_ext[:, j:j + 1, 0:HALF].to_broadcast([P, HEADS, HALF]), op=ALU.mult)
+            nc.vector.tensor_tensor(out=swapped[i][:, :, HALF:], in0=u[:, :, 0:HALF],
+                                    in1=sin_ext[:, j:j + 1, HALF:].to_broadcast([P, HEADS, HALF]), op=ALU.mult)
+
+        def apply_gain(pair):
+            h0 = chunks[2 * pair // ROW_TILES][3]
+            if h0 is None:
+                factor[pair] = rstd[pair]
+                return
+            factor[pair] = work.tile([P, 2 * HEADS], F32, name="factor", tag="factor", bufs=3)
+            nc.vector.tensor_tensor(out=factor[pair][:].rearrange("p (a h) -> p a h", a=2),
+                                    in0=rstd[pair][:].rearrange("p (a h) -> p a h", a=2),
+                                    in1=gain[:, h0:h0 + HEADS].unsqueeze(1).to_broadcast([P, 2, HEADS]), op=ALU.mult)
+
+        def cosine_terms(i):
+            pair, side = divmod(i, 2)
+            for h in range(HEADS):
+                col = side * HEADS + h
+                nc.vector.scalar_tensor_tensor(out=stage[i][:, h * HD:(h + 1) * HD], in0=acc[i][:, h * HD:(h + 1) * HD],
+                                               scalar=factor[pair][:, col:col + 1], in1=cos_ext[:, i % 2, :],
+                                               op0=ALU.mult, op1=ALU.mult)
+
+        def add_terms(i):
+            pair, side = divmod(i, 2)
+            for h in range(HEADS):
+                col = side * HEADS + h
+                rotary = stage[i][:, h * HD:h * HD + 2 * HALF]
+                nc.vector.scalar_tensor_tensor(out=rotary, in0=swapped[i][:, h, :],
+                                               scalar=factor[pair][:, col:col + 1], in1=rotary,
+                                               op0=ALU.mult, op1=ALU.add)
+            store(i)
+
+        n_units = len(units)
+        n_pairs = n_chunks * ROW_TILES // 2
+        first_close = PASSES
+        for tick in range(first_close + n_pairs + 1):
+            j0, j1 = 2 * tick, 2 * tick + 1
+            done = tick - first_close - 1
+            closing = tick - first_close
+            has_units = j0 < n_units
+            normed = done >= 0 and kind(2 * done) != "v"
+
+            if 0 <= j0 - 1 < n_units:
+                quantise(j0 - 1)
+            if has_units:
+                transpose_unit(j0)
+                transpose_unit(j1)
+            if done >= 0:
+                scalar_read(2 * done + 1)
+            if has_units:
+                drain(j0, 0)
+            if normed:
+                inverse_rms(done)
+            if has_units:
+                drain(j0, 1)
+                drain(j1, 0)
+                drain(j1, 1)
+            if normed:
+                sine_terms(2 * done)
+                sine_terms(2 * done + 1)
+                apply_gain(done)
+                cosine_terms(2 * done)
+            if has_units:
+                quantise(j0)
+            if normed:
+                cosine_terms(2 * done + 1)
+                add_terms(2 * done)
+                add_terms(2 * done + 1)
+
+            if 1 <= tick < first_close:
+                for i in range(ROW_TILES):
+                    multiply(i, tick - 1)
+            elif 0 <= closing < n_pairs:
+                for i in (2 * closing, 2 * closing + 1):
+                    for g in range(PASSES - 1 if i < ROW_TILES else 0, PASSES):
+                        multiply(i, g)
+                scalar_read(2 * closing)

@@ -19,23 +19,29 @@ ALU = mybir.AluOpType
 P = 128
 K_PASS = 512
 PASSES = DIM // K_PASS
-ROWS = 512
-ROW_TILES = ROWS // P
-HEADS = ROWS // HD
-WORDS = K_PASS // 2
+PAIRS = K_PASS // 2
+CHUNK = 512
+SLOTS = 4
+HEADS = CHUNK // HD
+TOKEN_TILES = B * S // P
+
+WHOLE_ROW_CHUNKS = 2
+PRESORT_END = 24
 
 
 def tile_causalselfattention_pa_kernel(tc, x, Wq, Wk, Wv, q_gain, cos_tab, sin_tab, out_0, out_1, out_2):
     nc = tc.nc
-    x2 = x.rearrange("b s k -> (b s) k")
-    q2 = out_0.rearrange("b s h d -> (b s) (h d)")
-    k2 = out_1.rearrange("b s h d -> (b s) (h d)")
-    v2 = out_2.rearrange("b s h d -> (b s) (h d)")
-    chunks = [("k", Wk, k2, None)]
+    x_tiles = x.rearrange("b (p j) k -> b j p k", j=2)
+    q_tiles = out_0.rearrange("b (p j) h d -> b j p (h d)", j=2)
+    k_tiles = out_1.rearrange("b (p j) h d -> b j p (h d)", j=2)
+    v_tiles = out_2.rearrange("b (p j) h d -> b j p (h d)", j=2)
+
+    chunks = [("k", Wk, k_tiles, None)]
     for c in range(H // HEADS):
-        chunks.append(("q", Wq[c * ROWS:(c + 1) * ROWS, :], q2[:, c * ROWS:(c + 1) * ROWS], c * HEADS))
-    chunks.append(("v", Wv, v2, None))
-    n_chunks = len(chunks)
+        features = slice(c * CHUNK, (c + 1) * CHUNK)
+        chunks.append(("q", Wq[features, :], q_tiles[:, :, :, features], c * HEADS))
+    chunks.append(("v", Wv, v_tiles, None))
+    n_out = len(chunks) * TOKEN_TILES
 
     with ExitStack() as ctx:
         keep = ctx.enter_context(tc.tile_pool(name="keep", bufs=1))
@@ -45,183 +51,228 @@ def tile_causalselfattention_pa_kernel(tc, x, Wq, Wk, Wv, q_gain, cos_tab, sin_t
 
         ident = keep.tile([P, P], F32, name="ident")
         make_identity(nc, ident[:])
-        cos_ext = keep.tile([P, 2, HD], F32, name="cos_ext")
-        sin_ext = keep.tile([P, 2, 2 * HALF], F32, name="sin_ext")
-        nc.gpsimd.memset(cos_ext[:, :, 2 * HALF:], 1.0)
+        cos_row = keep.tile([P, 2, HD], BF16, name="cos_row")
+        nc.gpsimd.memset(cos_row[:, :, 2 * HALF:], 1.0)
 
-        def load(name, rows, g0, n_pass):
-            raw = keep.tile([P, ROW_TILES, n_pass * K_PASS], BF16, name=name)
-            cols = slice(g0 * K_PASS, (g0 + n_pass) * K_PASS)
-            nc.sync.dma_start(out=raw[:], in_=rows[:, cols].rearrange("(r p) k -> p r k", p=P))
-            words = raw[:].bitcast(F32)
-            return [words[:, :, i * WORDS:(i + 1) * WORDS] for i in range(n_pass)]
+        warm_in = keep.tile([P, 1], F32, name="warm_in")
+        warm_out = keep.tile([P, 1], F32, name="warm_out")
+        nc.vector.memset(warm_in[:], 1.0)
+        nc.scalar.activation(out=warm_out[:], in_=warm_in[:], func=ACT.Abs_reciprocal_sqrt)
 
         units = []
-        for g in range(PASSES):
-            units.append((("x", g), load("x_raw%d" % g, x2, g, 1)[0]))
-            units.append(((0, g), load("w0_raw%d" % g, chunks[0][1], g, 1)[0]))
+
+        def load_whole_rows(operand, index, rows):
+            raw = keep.tile([P, DIM], BF16, name="rows_%s_%d" % (operand, index))
+            nc.sync.dma_start(out=raw[:], in_=rows)
+            units.append((operand, index, raw[:].bitcast(F32).rearrange("p (g w) -> p g w", g=PASSES)))
+
+        def load_two_passes(c, g0):
+            raw = keep.tile([P, SLOTS, 2 * K_PASS], BF16, name="passes_%d_%d" % (c, g0))
+            columns = chunks[c][1][:, g0 * K_PASS:(g0 + 2) * K_PASS]
+            nc.sync.dma_start(out=raw[:], in_=columns.rearrange("(r p) k -> p r k", p=P))
+            for n in range(2):
+                units.append((c, g0 + n, raw[:].bitcast(F32)[:, :, n * PAIRS:(n + 1) * PAIRS]))
+
+        def weight_rows(c, r):
+            return chunks[c][1][r * P:(r + 1) * P, :]
+
         cos_raw = keep.tile([P, 2, HALF], BF16, name="cos_raw")
         sin_raw = keep.tile([P, 2, HALF], BF16, name="sin_raw")
-        nc.sync.dma_start(out=cos_raw[:], in_=cos_tab.rearrange("(j p) d -> p j d", p=P))
-        nc.sync.dma_start(out=sin_raw[:], in_=sin_tab.rearrange("(j p) d -> p j d", p=P))
         gain = keep.tile([P, H], BF16, name="gain")
-        for c in range(1, n_chunks):
-            for g0 in (0, 2):
-                pair = load("w%d_raw%d" % (c, g0), chunks[c][1], g0, 2)
-                units.append(((c, g0), pair[0]))
-                units.append(((c, g0 + 1), pair[1]))
-            if c == 1:
-                nc.sync.dma_start(out=gain[:], in_=q_gain.partition_broadcast(P))
 
-        nc.gpsimd.tensor_copy(out=cos_ext[:, :, 0:HALF], in_=cos_raw[:])
-        nc.gpsimd.tensor_copy(out=cos_ext[:, :, HALF:2 * HALF], in_=cos_raw[:])
-        nc.gpsimd.tensor_copy(out=sin_ext[:, :, 0:HALF], in_=sin_raw[:])
-        nc.gpsimd.tensor_scalar(out=sin_ext[:, :, HALF:], in0=sin_raw[:], scalar1=-1.0, scalar2=0.0,
-                                op0=ALU.mult, op1=ALU.add)
+        load_whole_rows("x", 0, x_tiles[0, 0])
+        for r in range(SLOTS):
+            load_whole_rows(0, r, weight_rows(0, r))
+        for t in range(1, TOKEN_TILES):
+            load_whole_rows("x", t, x_tiles[t // 2, t % 2])
+        load_whole_rows(1, 0, weight_rows(1, 0))
+        nc.sync.dma_start(out=sin_raw[:], in_=sin_tab.rearrange("(p j) d -> p j d", j=2))
+        nc.sync.dma_start(out=cos_raw[:], in_=cos_tab.rearrange("(p j) d -> p j d", j=2))
+        for r in range(1, SLOTS):
+            load_whole_rows(1, r, weight_rows(1, r))
+        nc.sync.dma_start(out=gain[:], in_=q_gain.partition_broadcast(P))
+        for c in range(WHOLE_ROW_CHUNKS, len(chunks)):
+            for g0 in range(0, PASSES, 2):
+                load_two_passes(c, g0)
+        n_units = len(units)
 
-        banks, grouped, quantised = {}, {}, {}
-        acc, stage, swapped, ssq, rstd, factor = {}, {}, {}, {}, {}, {}
+        presorted, turned, grouped, quantised = {}, {}, {}, {}
 
-        def transpose_unit(j):
-            words = units[j][1]
-            for b in range(2):
-                bank = psum.tile([P, 2, 2, P], F32, name="bank", tag="bank")
-                banks[j, b] = bank
-                for r in range(2):
+        def presort(n):
+            if n < PRESORT_END and (n % 2 == 0 or n == 1):
+                presorted[n] = work.tile([P, SLOTS, 2, P], F32, name="presorted", bufs=4)
+                nc.vector.tensor_copy(out=presorted[n][:], in_=units[n][2].rearrange("p s (w u) -> p s u w", u=2))
+
+        def transpose_unit(n):
+            for half in range(2):
+                bank = psum.tile([P, 2, 2, P], F32, name="turned")
+                turned[n, half] = bank
+                for s in range(2):
+                    slot = 2 * half + s
                     for u in range(2):
-                        nc.tensor.transpose(bank[:, r, u, :], words[:, 2 * b + r, u:WORDS:2], ident[:])
+                        if n in presorted:
+                            source = presorted[n][:, slot, u, :]
+                        else:
+                            source = units[n][2][:, slot, u:PAIRS:2]
+                        nc.tensor.transpose(bank[:, s, u, :], source, ident[:])
 
-        def drain(j, b):
-            if b == 0:
-                grouped[j] = work.tile([P, 4 * ROWS], BF16, name="grouped", tag="grouped", bufs=4, align_bytes=64)
-            dst = grouped[j][:].bitcast(F32)[:, b * ROWS:(b + 1) * ROWS]
-            nc.scalar.copy(out=dst.rearrange("p (r n u) -> p r n u", r=2, u=2),
-                           in_=banks[j, b][:].rearrange("p r u n -> p r n u"))
+        def drain(n, half):
+            if half == 0:
+                grouped[n] = work.tile([P, SLOTS * P * 4], BF16, name="grouped", bufs=4, align_bytes=64)
+            target = grouped[n][:].bitcast(F32)[:, half * 4 * P:(half + 1) * 4 * P]
+            nc.scalar.copy(out=target.rearrange("p (s r u) -> p s r u", s=2, u=2),
+                           in_=turned[n, half][:].rearrange("p s u r -> p s r u"))
 
-        def quantise(j):
-            key = units[j][0]
-            tag, bufs = ("x", PASSES) if key[0] == "x" else ("w", 10)
-            codes = work.tile([P, ROWS], U32, name=tag + "_codes", tag=tag + "_codes", bufs=bufs, align_bytes=64)
-            scales = work.tile([P, ROWS], U8, name=tag + "_scales", tag=tag + "_scales", bufs=bufs, align_bytes=64)
-            nc.vector.quantize_mx(out=codes[:].bitcast(E5M2X4), scales=scales[:], in_=grouped[j][:])
-            quantised[key] = (codes, scales)
+        def operand_tiles(name, bufs):
+            codes = work.tile([P, SLOTS * P], U32, name=name + "_codes", bufs=bufs, align_bytes=64)
+            scales = work.tile([P, SLOTS * P], U8, name=name + "_scales", bufs=bufs, align_bytes=64)
+            return codes, scales
 
-        def multiply(i, g):
-            c, t = divmod(i, ROW_TILES)
-            if g == 0:
-                acc[i] = psum.tile([P, ROWS], F32, name="acc", tag="acc")
-            x_codes, x_scales = quantised["x", g]
-            w_codes, w_scales = quantised[c, g]
-            tokens = slice(t * P, (t + 1) * P)
-            nc.tensor.matmul_mx(out=acc[i][:], lhsT=x_codes[:, tokens].bitcast(E5M2X4), lhsT_scale=x_scales[:, tokens],
-                                rhs=w_codes[:].bitcast(E5M2X4), rhs_scale=w_scales[:],
-                                start=(g == 0), stop=(g == PASSES - 1))
+        def quantise(n):
+            operand, index = units[n][0], units[n][1]
+            if operand != "x" and operand < WHOLE_ROW_CHUNKS:
+                rows = slice(index * P, (index + 1) * P)
+                for g in range(PASSES):
+                    if index == 0:
+                        quantised[operand, g] = operand_tiles("w", 3 * PASSES)
+                    codes, scales = quantised[operand, g]
+                    nc.vector.quantize_mx(out=codes[:, rows].bitcast(E5M2X4), scales=scales[:, rows],
+                                          in_=grouped[n][:, g * 4 * P:(g + 1) * 4 * P])
+            else:
+                codes, scales = operand_tiles("x", TOKEN_TILES) if operand == "x" else operand_tiles("w", 3 * PASSES)
+                nc.vector.quantize_mx(out=codes[:].bitcast(E5M2X4), scales=scales[:], in_=grouped[n][:])
+                quantised[operand, index] = (codes, scales)
+
+        sums = {}
 
         def kind(i):
-            return chunks[i // ROW_TILES][0]
+            return chunks[i // TOKEN_TILES][0]
+
+        def multiply(i, features):
+            c, t = divmod(i, TOKEN_TILES)
+            if features.start == 0:
+                sums[i] = psum.tile([P, CHUNK], F32, name="turned" if kind(i) == "v" else "sums")
+            x_codes, x_scales = quantised["x", t]
+            for g in range(PASSES):
+                w_codes, w_scales = quantised[c, g]
+                tokens = slice(g * P, (g + 1) * P)
+                nc.tensor.matmul_mx(out=sums[i][:, features],
+                                    lhsT=x_codes[:, tokens].bitcast(E5M2X4), lhsT_scale=x_scales[:, tokens],
+                                    rhs=w_codes[:, features].bitcast(E5M2X4), rhs_scale=w_scales[:, features],
+                                    start=(g == 0), stop=(g == PASSES - 1))
+
+        result, sine, squares, factor = {}, {}, {}, {}
 
         def store(i):
-            c, t = divmod(i, ROW_TILES)
-            nc.sync.dma_start(out=chunks[c][2][t * P:(t + 1) * P, :], in_=stage[i][:])
+            c, t = divmod(i, TOKEN_TILES)
+            queue = nc.scalar if kind(i) == "v" else nc.sync
+            queue.dma_start(out=chunks[c][2][t // 2, t % 2], in_=result[i][:])
 
         def scalar_read(i):
-            stage[i] = work.tile([P, ROWS], F32, name="stage", tag="stage", bufs=12)
+            result[i] = work.tile([P, CHUNK], F32, name="result", bufs=12)
             if kind(i) == "v":
-                nc.scalar.copy(out=stage[i][:], in_=acc[i][:])
+                nc.scalar.copy(out=result[i][:], in_=sums[i][:])
                 store(i)
                 return
-            pair, side = divmod(i, 2)
+            couple, side = divmod(i, 2)
             if side == 0:
-                ssq[pair] = work.tile([P, 2 * HEADS], F32, name="ssq", tag="ssq", bufs=3)
+                squares[couple] = work.tile([P, 2 * HEADS], F32, name="squares", bufs=3)
             for h in range(HEADS):
-                col = side * HEADS + h
-                nc.scalar.activation(out=stage[i][:, h * HD:(h + 1) * HD], in_=acc[i][:, h * HD:(h + 1) * HD],
-                                     func=ACT.Square, accum_out=ssq[pair][:, col:col + 1])
+                head, column = slice(h * HD, (h + 1) * HD), side * HEADS + h
+                nc.scalar.activation(out=result[i][:, head], in_=sums[i][:, head], func=ACT.Square,
+                                     accum_out=squares[couple][:, column:column + 1])
 
-        def inverse_rms(pair):
-            rstd[pair] = work.tile([P, 2 * HEADS], F32, name="rstd", tag="rstd", bufs=3)
-            nc.scalar.activation(out=rstd[pair][:], in_=ssq[pair][:], func=ACT.Abs_reciprocal_sqrt,
+        def inverse_rms(couple):
+            factor[couple] = work.tile([P, 2 * HEADS], F32, name="inverse_rms", bufs=3)
+            nc.scalar.activation(out=factor[couple][:], in_=squares[couple][:], func=ACT.Abs_reciprocal_sqrt,
                                  scale=1.0 / HD, bias=EPS)
 
-        def sine_terms(i):
-            j = i % 2
-            u = acc[i][:].rearrange("p (h d) -> p h d", h=HEADS)
-            swapped[i] = work.tile([P, HEADS, 2 * HALF], F32, name="swapped", tag="swapped", bufs=4)
-            nc.vector.tensor_tensor(out=swapped[i][:, :, 0:HALF], in0=u[:, :, HALF:2 * HALF],
-                                    in1=sin_ext[:, j:j + 1, 0:HALF].to_broadcast([P, HEADS, HALF]), op=ALU.mult)
-            nc.vector.tensor_tensor(out=swapped[i][:, :, HALF:], in0=u[:, :, 0:HALF],
-                                    in1=sin_ext[:, j:j + 1, HALF:].to_broadcast([P, HEADS, HALF]), op=ALU.mult)
+        def apply_gain(couple):
+            first = chunks[2 * couple // TOKEN_TILES][3]
+            if first is not None:
+                plain = factor[couple]
+                factor[couple] = work.tile([P, 2 * HEADS], F32, name="gained", bufs=3)
+                nc.vector.tensor_tensor(out=factor[couple][:].rearrange("p (a h) -> p a h", a=2),
+                                        in0=plain[:].rearrange("p (a h) -> p a h", a=2),
+                                        in1=gain[:, first:first + HEADS].unsqueeze(1).to_broadcast([P, 2, HEADS]),
+                                        op=ALU.mult)
 
-        def apply_gain(pair):
-            h0 = chunks[2 * pair // ROW_TILES][3]
-            if h0 is None:
-                factor[pair] = rstd[pair]
-                return
-            factor[pair] = work.tile([P, 2 * HEADS], F32, name="factor", tag="factor", bufs=3)
-            nc.vector.tensor_tensor(out=factor[pair][:].rearrange("p (a h) -> p a h", a=2),
-                                    in0=rstd[pair][:].rearrange("p (a h) -> p a h", a=2),
-                                    in1=gain[:, h0:h0 + HEADS].unsqueeze(1).to_broadcast([P, 2, HEADS]), op=ALU.mult)
+        def sine_terms(i):
+            u = sums[i][:].rearrange("p (h d) -> p h d", h=HEADS)
+            sin_heads = sin_raw[:, i % 2:i % 2 + 1, :].to_broadcast([P, HEADS, HALF])
+            sine[i] = work.tile([P, HEADS, 2 * HALF], F32, name="sine", bufs=4)
+            nc.vector.tensor_tensor(out=sine[i][:, :, 0:HALF], in0=u[:, :, HALF:2 * HALF], in1=sin_heads, op=ALU.mult)
+            nc.vector.scalar_tensor_tensor(out=sine[i][:, :, HALF:], in0=u[:, :, 0:HALF], scalar=-1.0, in1=sin_heads,
+                                           op0=ALU.mult, op1=ALU.mult)
 
         def cosine_terms(i):
-            pair, side = divmod(i, 2)
+            couple, side = divmod(i, 2)
             for h in range(HEADS):
-                col = side * HEADS + h
-                nc.vector.scalar_tensor_tensor(out=stage[i][:, h * HD:(h + 1) * HD], in0=acc[i][:, h * HD:(h + 1) * HD],
-                                               scalar=factor[pair][:, col:col + 1], in1=cos_ext[:, i % 2, :],
+                head, column = slice(h * HD, (h + 1) * HD), side * HEADS + h
+                nc.vector.scalar_tensor_tensor(out=result[i][:, head], in0=sums[i][:, head],
+                                               scalar=factor[couple][:, column:column + 1], in1=cos_row[:, i % 2, :],
                                                op0=ALU.mult, op1=ALU.mult)
 
-        def add_terms(i):
-            pair, side = divmod(i, 2)
+        def add_sine_terms(i):
+            couple, side = divmod(i, 2)
             for h in range(HEADS):
-                col = side * HEADS + h
-                rotary = stage[i][:, h * HD:h * HD + 2 * HALF]
-                nc.vector.scalar_tensor_tensor(out=rotary, in0=swapped[i][:, h, :],
-                                               scalar=factor[pair][:, col:col + 1], in1=rotary,
+                rotated, column = result[i][:, h * HD:h * HD + 2 * HALF], side * HEADS + h
+                nc.vector.scalar_tensor_tensor(out=rotated, in0=sine[i][:, h, :],
+                                               scalar=factor[couple][:, column:column + 1], in1=rotated,
                                                op0=ALU.mult, op1=ALU.add)
             store(i)
 
-        n_units = len(units)
-        n_pairs = n_chunks * ROW_TILES // 2
-        first_close = PASSES
-        for tick in range(first_close + n_pairs + 1):
-            j0, j1 = 2 * tick, 2 * tick + 1
-            done = tick - first_close - 1
-            closing = tick - first_close
-            has_units = j0 < n_units
-            normed = done >= 0 and kind(2 * done) != "v"
+        whole = slice(0, CHUNK)
+        plan = {step: [] for step in range(n_out // 2 + 5)}
+        for r in range(SLOTS):
+            plan[(r + 1) // 2 + 1].append((0, slice(r * P, (r + 1) * P)))
+        for i in range(1, n_out):
+            plan[i + 2 if i < TOKEN_TILES else i // 2 + 4].append((i, whole))
+        finished = {step + 1: i // 2 for step in plan for i, features in plan[step] if i % 2 == 1}
 
-            if 0 <= j0 - 1 < n_units:
-                quantise(j0 - 1)
-            if has_units:
-                transpose_unit(j0)
-                transpose_unit(j1)
-            if done >= 0:
-                scalar_read(2 * done + 1)
-            if has_units:
-                drain(j0, 0)
-            if normed:
-                inverse_rms(done)
-            if has_units:
-                drain(j0, 1)
-                drain(j1, 0)
-                drain(j1, 1)
-            if normed:
-                sine_terms(2 * done)
-                sine_terms(2 * done + 1)
-                apply_gain(done)
-                cosine_terms(2 * done)
-            if has_units:
-                quantise(j0)
-            if normed:
-                cosine_terms(2 * done + 1)
-                add_terms(2 * done)
-                add_terms(2 * done + 1)
+        presort(0)
+        presort(1)
+        for step in sorted(plan):
+            first, second = 2 * step, 2 * step + 1
+            has_units = first < n_units
+            couple = finished.get(step)
+            normed = couple is not None and kind(2 * couple) != "v"
 
-            if 1 <= tick < first_close:
-                for i in range(ROW_TILES):
-                    multiply(i, tick - 1)
-            elif 0 <= closing < n_pairs:
-                for i in (2 * closing, 2 * closing + 1):
-                    for g in range(PASSES - 1 if i < ROW_TILES else 0, PASSES):
-                        multiply(i, g)
-                scalar_read(2 * closing)
+            if 0 <= first - 1 < n_units - 1:
+                quantise(first - 1)
+            presort(first + 2)
+            if has_units:
+                transpose_unit(first)
+                transpose_unit(second)
+            if couple is not None:
+                scalar_read(2 * couple + 1)
+            if has_units:
+                drain(first, 0)
+            if normed:
+                inverse_rms(couple)
+            if has_units:
+                drain(first, 1)
+                drain(second, 0)
+            if couple == 0:
+                nc.vector.tensor_copy(out=cos_row[:, :, 0:2 * HALF].rearrange("p j (a d) -> p j a d", a=2),
+                                      in_=cos_raw[:].unsqueeze(2).to_broadcast([P, 2, 2, HALF]))
+            if normed:
+                sine_terms(2 * couple)
+                sine_terms(2 * couple + 1)
+                apply_gain(couple)
+            if has_units:
+                quantise(first)
+                drain(second, 1)
+            if normed:
+                cosine_terms(2 * couple)
+            if second == n_units - 1:
+                quantise(second)
+            if normed:
+                cosine_terms(2 * couple + 1)
+                add_sine_terms(2 * couple)
+                add_sine_terms(2 * couple + 1)
+
+            for i, features in plan[step]:
+                multiply(i, features)
+                if features.stop == CHUNK and i % 2 == 0:
+                    scalar_read(i)

from contextlib import ExitStack

import concourse.mybir as mybir
from concourse.masks import make_identity

B, S, DIM, H, HKV, HD = 2, 256, 2048, 16, 4, 128
HALF = 32
EPS = 1.1920929e-07
FLOPS = 2 * B * S * DIM * (H + 2 * HKV) * HD

F32 = mybir.dt.float32
BF16 = mybir.dt.bfloat16
U32 = mybir.dt.uint32
U8 = mybir.dt.uint8
E5M2X4 = mybir.dt.float8_e5m2_x4
ACT = mybir.ActivationFunctionType
ALU = mybir.AluOpType

P = 128
K_PASS = 512
PASSES = DIM // K_PASS
PAIRS = K_PASS // 2
CHUNK = 512
SLOTS = 4
HEADS = CHUNK // HD
TOKEN_TILES = B * S // P

WHOLE_ROW_CHUNKS = 2
PRESORT_END = 24


def tile_causalselfattention_pa_kernel(tc, x, Wq, Wk, Wv, q_gain, cos_tab, sin_tab, out_0, out_1, out_2):
    nc = tc.nc
    x_tiles = x.rearrange("b (p j) k -> b j p k", j=2)
    q_tiles = out_0.rearrange("b (p j) h d -> b j p (h d)", j=2)
    k_tiles = out_1.rearrange("b (p j) h d -> b j p (h d)", j=2)
    v_tiles = out_2.rearrange("b (p j) h d -> b j p (h d)", j=2)

    chunks = [("k", Wk, k_tiles, None)]
    for c in range(H // HEADS):
        features = slice(c * CHUNK, (c + 1) * CHUNK)
        chunks.append(("q", Wq[features, :], q_tiles[:, :, :, features], c * HEADS))
    chunks.append(("v", Wv, v_tiles, None))
    n_out = len(chunks) * TOKEN_TILES

    with ExitStack() as ctx:
        keep = ctx.enter_context(tc.tile_pool(name="keep", bufs=1))
        work = ctx.enter_context(tc.tile_pool(name="work", bufs=1))
        psum = ctx.enter_context(tc.psum_pool(name="psum", bufs=4))
        ctx.enter_context(tc.manual_schedule())

        ident = keep.tile([P, P], F32, name="ident")
        make_identity(nc, ident[:])
        cos_row = keep.tile([P, 2, HD], BF16, name="cos_row")
        nc.gpsimd.memset(cos_row[:, :, 2 * HALF:], 1.0)

        warm_in = keep.tile([P, 1], F32, name="warm_in")
        warm_out = keep.tile([P, 1], F32, name="warm_out")
        nc.vector.memset(warm_in[:], 1.0)
        nc.scalar.activation(out=warm_out[:], in_=warm_in[:], func=ACT.Abs_reciprocal_sqrt)

        units = []

        def load_whole_rows(operand, index, rows):
            raw = keep.tile([P, DIM], BF16, name="rows_%s_%d" % (operand, index))
            nc.sync.dma_start(out=raw[:], in_=rows)
            units.append((operand, index, raw[:].bitcast(F32).rearrange("p (g w) -> p g w", g=PASSES)))

        def load_two_passes(c, g0):
            raw = keep.tile([P, SLOTS, 2 * K_PASS], BF16, name="passes_%d_%d" % (c, g0))
            columns = chunks[c][1][:, g0 * K_PASS:(g0 + 2) * K_PASS]
            nc.sync.dma_start(out=raw[:], in_=columns.rearrange("(r p) k -> p r k", p=P))
            for n in range(2):
                units.append((c, g0 + n, raw[:].bitcast(F32)[:, :, n * PAIRS:(n + 1) * PAIRS]))

        def weight_rows(c, r):
            return chunks[c][1][r * P:(r + 1) * P, :]

        cos_raw = keep.tile([P, 2, HALF], BF16, name="cos_raw")
        sin_raw = keep.tile([P, 2, HALF], BF16, name="sin_raw")
        gain = keep.tile([P, H], BF16, name="gain")

        load_whole_rows("x", 0, x_tiles[0, 0])
        for r in range(SLOTS):
            load_whole_rows(0, r, weight_rows(0, r))
        for t in range(1, TOKEN_TILES):
            load_whole_rows("x", t, x_tiles[t // 2, t % 2])
        load_whole_rows(1, 0, weight_rows(1, 0))
        nc.sync.dma_start(out=sin_raw[:], in_=sin_tab.rearrange("(p j) d -> p j d", j=2))
        nc.sync.dma_start(out=cos_raw[:], in_=cos_tab.rearrange("(p j) d -> p j d", j=2))
        for r in range(1, SLOTS):
            load_whole_rows(1, r, weight_rows(1, r))
        nc.sync.dma_start(out=gain[:], in_=q_gain.partition_broadcast(P))
        for c in range(WHOLE_ROW_CHUNKS, len(chunks)):
            for g0 in range(0, PASSES, 2):
                load_two_passes(c, g0)
        n_units = len(units)

        presorted, turned, grouped, quantised = {}, {}, {}, {}

        def presort(n):
            if n < PRESORT_END and (n % 2 == 0 or n == 1):
                presorted[n] = work.tile([P, SLOTS, 2, P], F32, name="presorted", bufs=4)
                nc.vector.tensor_copy(out=presorted[n][:], in_=units[n][2].rearrange("p s (w u) -> p s u w", u=2))

        def transpose_unit(n):
            for half in range(2):
                bank = psum.tile([P, 2, 2, P], F32, name="turned")
                turned[n, half] = bank
                for s in range(2):
                    slot = 2 * half + s
                    for u in range(2):
                        if n in presorted:
                            source = presorted[n][:, slot, u, :]
                        else:
                            source = units[n][2][:, slot, u:PAIRS:2]
                        nc.tensor.transpose(bank[:, s, u, :], source, ident[:])

        def drain(n, half):
            if half == 0:
                grouped[n] = work.tile([P, SLOTS * P * 4], BF16, name="grouped", bufs=4, align_bytes=64)
            target = grouped[n][:].bitcast(F32)[:, half * 4 * P:(half + 1) * 4 * P]
            nc.scalar.copy(out=target.rearrange("p (s r u) -> p s r u", s=2, u=2),
                           in_=turned[n, half][:].rearrange("p s u r -> p s r u"))

        def operand_tiles(name, bufs):
            codes = work.tile([P, SLOTS * P], U32, name=name + "_codes", bufs=bufs, align_bytes=64)
            scales = work.tile([P, SLOTS * P], U8, name=name + "_scales", bufs=bufs, align_bytes=64)
            return codes, scales

        def quantise(n):
            operand, index = units[n][0], units[n][1]
            if operand != "x" and operand < WHOLE_ROW_CHUNKS:
                rows = slice(index * P, (index + 1) * P)
                for g in range(PASSES):
                    if index == 0:
                        quantised[operand, g] = operand_tiles("w", 3 * PASSES)
                    codes, scales = quantised[operand, g]
                    nc.vector.quantize_mx(out=codes[:, rows].bitcast(E5M2X4), scales=scales[:, rows],
                                          in_=grouped[n][:, g * 4 * P:(g + 1) * 4 * P])
            else:
                codes, scales = operand_tiles("x", TOKEN_TILES) if operand == "x" else operand_tiles("w", 3 * PASSES)
                nc.vector.quantize_mx(out=codes[:].bitcast(E5M2X4), scales=scales[:], in_=grouped[n][:])
                quantised[operand, index] = (codes, scales)

        sums = {}

        def kind(i):
            return chunks[i // TOKEN_TILES][0]

        def multiply(i, features):
            c, t = divmod(i, TOKEN_TILES)
            if features.start == 0:
                sums[i] = psum.tile([P, CHUNK], F32, name="turned" if kind(i) == "v" else "sums")
            x_codes, x_scales = quantised["x", t]
            for g in range(PASSES):
                w_codes, w_scales = quantised[c, g]
                tokens = slice(g * P, (g + 1) * P)
                nc.tensor.matmul_mx(out=sums[i][:, features],
                                    lhsT=x_codes[:, tokens].bitcast(E5M2X4), lhsT_scale=x_scales[:, tokens],
                                    rhs=w_codes[:, features].bitcast(E5M2X4), rhs_scale=w_scales[:, features],
                                    start=(g == 0), stop=(g == PASSES - 1))

        result, sine, squares, factor = {}, {}, {}, {}

        def store(i):
            c, t = divmod(i, TOKEN_TILES)
            queue = nc.scalar if kind(i) == "v" else nc.sync
            queue.dma_start(out=chunks[c][2][t // 2, t % 2], in_=result[i][:])

        def scalar_read(i):
            result[i] = work.tile([P, CHUNK], F32, name="result", bufs=12)
            if kind(i) == "v":
                nc.scalar.copy(out=result[i][:], in_=sums[i][:])
                store(i)
                return
            couple, side = divmod(i, 2)
            if side == 0:
                squares[couple] = work.tile([P, 2 * HEADS], F32, name="squares", bufs=3)
            for h in range(HEADS):
                head, column = slice(h * HD, (h + 1) * HD), side * HEADS + h
                nc.scalar.activation(out=result[i][:, head], in_=sums[i][:, head], func=ACT.Square,
                                     accum_out=squares[couple][:, column:column + 1])

        def inverse_rms(couple):
            factor[couple] = work.tile([P, 2 * HEADS], F32, name="inverse_rms", bufs=3)
            nc.scalar.activation(out=factor[couple][:], in_=squares[couple][:], func=ACT.Abs_reciprocal_sqrt,
                                 scale=1.0 / HD, bias=EPS)

        def apply_gain(couple):
            first = chunks[2 * couple // TOKEN_TILES][3]
            if first is not None:
                plain = factor[couple]
                factor[couple] = work.tile([P, 2 * HEADS], F32, name="gained", bufs=3)
                nc.vector.tensor_tensor(out=factor[couple][:].rearrange("p (a h) -> p a h", a=2),
                                        in0=plain[:].rearrange("p (a h) -> p a h", a=2),
                                        in1=gain[:, first:first + HEADS].unsqueeze(1).to_broadcast([P, 2, HEADS]),
                                        op=ALU.mult)

        def sine_terms(i):
            u = sums[i][:].rearrange("p (h d) -> p h d", h=HEADS)
            sin_heads = sin_raw[:, i % 2:i % 2 + 1, :].to_broadcast([P, HEADS, HALF])
            sine[i] = work.tile([P, HEADS, 2 * HALF], F32, name="sine", bufs=4)
            nc.vector.tensor_tensor(out=sine[i][:, :, 0:HALF], in0=u[:, :, HALF:2 * HALF], in1=sin_heads, op=ALU.mult)
            nc.vector.scalar_tensor_tensor(out=sine[i][:, :, HALF:], in0=u[:, :, 0:HALF], scalar=-1.0, in1=sin_heads,
                                           op0=ALU.mult, op1=ALU.mult)

        def cosine_terms(i):
            couple, side = divmod(i, 2)
            for h in range(HEADS):
                head, column = slice(h * HD, (h + 1) * HD), side * HEADS + h
                nc.vector.scalar_tensor_tensor(out=result[i][:, head], in0=sums[i][:, head],
                                               scalar=factor[couple][:, column:column + 1], in1=cos_row[:, i % 2, :],
                                               op0=ALU.mult, op1=ALU.mult)

        def add_sine_terms(i):
            couple, side = divmod(i, 2)
            for h in range(HEADS):
                rotated, column = result[i][:, h * HD:h * HD + 2 * HALF], side * HEADS + h
                nc.vector.scalar_tensor_tensor(out=rotated, in0=sine[i][:, h, :],
                                               scalar=factor[couple][:, column:column + 1], in1=rotated,
                                               op0=ALU.mult, op1=ALU.add)
            store(i)

        whole = slice(0, CHUNK)
        plan = {step: [] for step in range(n_out // 2 + 5)}
        for r in range(SLOTS):
            plan[(r + 1) // 2 + 1].append((0, slice(r * P, (r + 1) * P)))
        for i in range(1, n_out):
            plan[i + 2 if i < TOKEN_TILES else i // 2 + 4].append((i, whole))
        finished = {step + 1: i // 2 for step in plan for i, features in plan[step] if i % 2 == 1}

        presort(0)
        presort(1)
        for step in sorted(plan):
            first, second = 2 * step, 2 * step + 1
            has_units = first < n_units
            couple = finished.get(step)
            normed = couple is not None and kind(2 * couple) != "v"

            if 0 <= first - 1 < n_units - 1:
                quantise(first - 1)
            presort(first + 2)
            if has_units:
                transpose_unit(first)
                transpose_unit(second)
            if couple is not None:
                scalar_read(2 * couple + 1)
            if has_units:
                drain(first, 0)
            if normed:
                inverse_rms(couple)
            if has_units:
                drain(first, 1)
                drain(second, 0)
            if couple == 0:
                nc.vector.tensor_copy(out=cos_row[:, :, 0:2 * HALF].rearrange("p j (a d) -> p j a d", a=2),
                                      in_=cos_raw[:].unsqueeze(2).to_broadcast([P, 2, 2, HALF]))
            if normed:
                sine_terms(2 * couple)
                sine_terms(2 * couple + 1)
                apply_gain(couple)
            if has_units:
                quantise(first)
                drain(second, 1)
            if normed:
                cosine_terms(2 * couple)
            if second == n_units - 1:
                quantise(second)
            if normed:
                cosine_terms(2 * couple + 1)
                add_sine_terms(2 * couple)
                add_sine_terms(2 * couple + 1)

            for i, features in plan[step]:
                multiply(i, features)
                if features.stop == CHUNK and i % 2 == 0:
                    scalar_read(i)
